import numpy as np
import ml_dtypes


def mxq(x, axis, fmt="e4m3"):
    dtype, down = {"e4m3": (ml_dtypes.float8_e4m3fn, 7), "e5m2": (ml_dtypes.float8_e5m2, 14)}[fmt]
    v = np.moveaxis(np.asarray(x, np.float32).astype(ml_dtypes.bfloat16).astype(np.float64), axis, -1)
    blocks = v.reshape(v.shape[:-1] + (-1, 32))
    amax = np.abs(blocks).max(-1, keepdims=True)
    byte = np.maximum(np.where(amax > 0, np.frexp(amax)[1] - 1 + 127, 0) - down, 1)
    scale = np.exp2(byte - 127.0)
    codes = (blocks / scale).astype(np.float32).astype(dtype).astype(np.float64)
    return np.moveaxis((codes * scale).reshape(v.shape), -1, axis)


WIDE = False


def mx_kscale(k):
    if not WIDE:
        return np.ones(k)
    levels = np.array([10, -10, 5, -5, 0])
    a = np.random.permutation(np.resize(levels, k // 512 * 4)).reshape(k // 512, 4)
    idx = np.arange(k)
    return np.exp2(a[idx // 512, idx % 128 // 32])


BF16 = ml_dtypes.bfloat16


def bf(x):
    return np.asarray(x, np.float32).astype(BF16)


def f64(x):
    return np.asarray(x).astype(np.float64)


E2M1 = np.array([0.0, 0.5, 1.0, 1.5, 2.0, 3.0, 4.0, 6.0, -0.0, -0.5, -1.0, -1.5, -2.0, -3.0, -4.0, -6.0])


def pack_weight(w, fmt):
    k, n = w.shape
    w = f64(bf(w)).reshape(k // 32, 32, n)
    amax = np.abs(w).max(1)
    if fmt == "e4m3":
        byte = np.frexp(amax)[1] - 1 + 127 - 7
    else:
        mant, ex = np.frexp(amax / 6.0)
        byte = np.where(mant > 0.5, ex, ex - 1) + 127
    byte = np.clip(np.where(amax > 0, byte, 1), 1, 254)
    scaled = (w * np.exp2(127.0 - byte)[:, None, :]).reshape(k, n).astype(np.float32)
    by_word = np.ascontiguousarray(scaled.reshape(k // 512, 128, 4, n).transpose(0, 1, 3, 2))
    if fmt == "e4m3":
        words = by_word.astype(ml_dtypes.float8_e4m3fn).view(np.uint8)
    else:
        c = by_word.astype(ml_dtypes.float4_e2m1fn).view(np.uint8) & 0xF
        words = c[..., 0::2] | (c[..., 1::2] << 4)
    return np.ascontiguousarray(words), np.ascontiguousarray(byte.astype(np.uint8).reshape(k // 512, 16, n))


def unpack_weight(words, scales, fmt):
    g, p, n, _ = words.shape
    if fmt == "e4m3":
        vals = np.ascontiguousarray(words).view(ml_dtypes.float8_e4m3fn).astype(np.float64)
    else:
        nib = np.empty((g, p, n, 4), np.uint8)
        nib[..., 0::2] = words & 0xF
        nib[..., 1::2] = words >> 4
        vals = E2M1[nib]
    vals = vals * np.repeat(np.exp2(scales.astype(np.float64) - 127.0), 8, axis=1)[..., None]
    return vals.transpose(0, 1, 3, 2).reshape(g * 512, n)


B, S, H, HD = 1, 512, 2048, 128
NH = H // HD
HALF = HD // 2
WS = 1.5 * (HD / H) ** 0.25 / np.sqrt(H)
FMT = "e4m3"


def rotate_half(u):
    return np.concatenate((-u[..., HALF:], u[..., :HALF]), axis=-1)


def rope(u, c, s):
    u4 = u.reshape(B, S, NH, HD)
    return (u4 * c[None, :, None, :] + rotate_half(u4) * s[None, :, None, :]).reshape(B, S, H)


def setup_inputs():
    s = mx_kscale(H)
    t = np.tile(mx_kscale(H).reshape(NH, 2, HALF)[:, :1, :], (1, 2, 1)).reshape(H)
    hidden_states = bf(np.random.standard_normal((B, S, H)) * s)
    wq = np.random.standard_normal((H, H)) * WS * t[:, None] / s[None, :]
    wk = np.random.standard_normal((H, H)) * WS / t[:, None] / s[None, :]
    wq_words, wq_scales = pack_weight(np.ascontiguousarray(wq.T), FMT)
    wk_words, wk_scales = pack_weight(np.ascontiguousarray(wk.T), FMT)
    return {"hidden_states": hidden_states,
            "wq_deq_words": wq_words,
            "wq_deq_scales": wq_scales,
            "wk_deq_words": wk_words,
            "wk_deq_scales": wk_scales,
            "cos": bf(np.random.random((S, HD))),
            "sin": bf(np.random.random((S, HD))),
            "attention_mask": bf(np.random.standard_normal((1, S, S)) * 0.5)}


def reference(hidden_states, wq_deq_words, wq_deq_scales, wk_deq_words, wk_deq_scales, cos, sin, attention_mask):
    xq = mxq(f64(hidden_states), 2, "e4m3")
    q = xq @ unpack_weight(wq_deq_words, wq_deq_scales, FMT)
    k = xq @ unpack_weight(wk_deq_words, wk_deq_scales, FMT)
    q_rot = rope(q, f64(cos), f64(sin))
    k_rot = rope(k, f64(cos), f64(sin))
    scores = (mxq(q_rot, 2, "e4m3") @ mxq(k_rot, 2, "e4m3").transpose(0, 2, 1)) / np.sqrt(HD)
    return scores + f64(attention_mask)

@@ -1,0 +1,252 @@
+import math
+from contextlib import ExitStack
+
+import concourse.mybir as mybir
+from concourse.masks import make_identity
+
+F32 = mybir.dt.float32
+BF16 = mybir.dt.bfloat16
+I32 = mybir.dt.int32
+U32 = mybir.dt.uint32
+U8 = mybir.dt.uint8
+FP8X4 = mybir.dt.float8_e4m3fn_x4
+MULT = mybir.AluOpType.mult
+ADD = mybir.AluOpType.add
+
+P = 128
+TOKENS = 512
+HIDDEN = 2048
+CHUNK = 128
+HALF = CHUNK // 2
+N_CHUNKS = HIDDEN // CHUNK
+K_PASS = 4 * P
+PASSES = HIDDEN // K_PASS
+TOKEN_TILES = TOKENS // P
+BLOCK = 256
+BLOCKS = TOKENS // BLOCK
+TILES_PER_BLOCK = BLOCK // P
+GROUPS = PASSES
+PAIRS = 2
+
+FLOPS = 2 * (2 * TOKENS * HIDDEN * HIDDEN) + 2 * TOKENS * TOKENS * HIDDEN
+
+
+def tile_llamaattention_pa_kernel(
+    tc, hidden_states, wq_words, wq_scales, wk_words, wk_scales, cos, sin, attention_mask, out
+):
+    nc = tc.nc
+    weights_dram = ((wk_words, wk_scales), (wq_words, wq_scales))
+
+    with ExitStack() as ctx:
+        keep = ctx.enter_context(tc.tile_pool(name="keep", bufs=1))
+        work = ctx.enter_context(tc.tile_pool(name="work", bufs=3))
+        psum = ctx.enter_context(tc.psum_pool(name="psum", bufs=8))
+        ctx.enter_context(tc.manual_schedule())
+
+        ident = keep.tile([P, P], F32)
+        make_identity(nc, ident[:])
+
+        cos_sb = keep.tile([P, TOKEN_TILES, CHUNK], BF16)
+        sin_sb = keep.tile([P, TOKEN_TILES, CHUNK], BF16)
+        nc.scalar.dma_start(out=cos_sb[:], in_=cos.rearrange("(t p) f -> p t f", p=P))
+        nc.scalar.dma_start(out=sin_sb[:], in_=sin.rearrange("(t p) f -> p t f", p=P))
+
+        staged = []
+        for w in range(2):
+            stage = keep.tile([P, HIDDEN], U8, name="stage%d" % w, align_bytes=64)
+            nc.vector.memset(stage[:].bitcast(I32), 0)
+            for quad in range(4):
+                nc.sync.dma_start(
+                    out=stage[32 * quad : 32 * quad + 16, :].bitcast(I32),
+                    in_=weights_dram[w][1][:, 4 * quad : 4 * quad + 4, :].bitcast(I32),
+                )
+            staged.append(stage)
+
+        x_sb = []
+        for t in range(TOKEN_TILES):
+            x_t = keep.tile([P, HIDDEN], BF16, name="x%d" % t)
+            nc.sync.dma_start(out=x_t[:], in_=hidden_states[0, t * P : (t + 1) * P, :])
+            x_sb.append(x_t)
+
+        w_sb = []
+        for w in range(2):
+            per_group = []
+            for grp in range(GROUPS):
+                w_g = keep.tile([P, PASSES, 2, 4 * HALF], U32, name="w%d_%d" % (w, grp), align_bytes=64)
+                for half in range(2):
+                    for kp in range(PASSES):
+                        words = weights_dram[w][0][kp].rearrange("p n t -> p (n t)").bitcast(I32)
+                        nc.sync.dma_start(
+                            out=w_g[:, kp, half, :].bitcast(I32).rearrange("p (c i) -> p c i", i=HALF),
+                            in_=words.rearrange("p (c h i) -> p c h i", h=2, i=HALF)[
+                                :, 4 * grp : 4 * grp + 4, half, :
+                            ],
+                        )
+                per_group.append(w_g)
+            w_sb.append(per_group)
+
+        mask_sb = keep.tile([P, TOKEN_TILES, TOKENS], BF16)
+        nc.sync.dma_start(out=mask_sb[:], in_=attention_mask[0].rearrange("(t p) s -> p t s", p=P))
+
+        table_src = keep.tile([P, TOKEN_TILES, 4, CHUNK], F32)
+        twice = [P, TOKEN_TILES, 2, HALF]
+        sources = (cos_sb[:, :, 0:HALF], sin_sb[:, :, HALF:CHUNK], sin_sb[:, :, 0:HALF], cos_sb[:, :, HALF:CHUNK])
+        for k in range(4):
+            nc.vector.tensor_scalar_mul(
+                out=table_src[:, :, k, :].rearrange("p t (d i) -> p t d i", d=2),
+                in0=sources[k].unsqueeze(2).to_broadcast(twice),
+                scalar1=(-1.0 if k == 2 else 1.0),
+            )
+
+        planes = []
+        for w in range(2):
+            plane = keep.tile([P, HIDDEN], U8, name="plane%d" % w, align_bytes=64)
+            nc.vector.tensor_copy(
+                out=plane[:].bitcast(I32).rearrange("p (h c i) -> p h c i", h=2, c=N_CHUNKS),
+                in_=staged[w][:].bitcast(I32).rearrange("p (c h i) -> p h c i", h=2, c=N_CHUNKS),
+            )
+            planes.append(plane)
+
+        x_codes = []
+        x_scales = []
+
+        def quantise_x(blk):
+            banks = [psum.tile([P, 2, BLOCK], F32, name="bank") for kp in range(PASSES)]
+            for tt in range(TILES_PER_BLOCK):
+                x_words = x_sb[blk * TILES_PER_BLOCK + tt][:].bitcast(F32)
+                for kp in range(PASSES):
+                    for u in range(2):
+                        nc.tensor.transpose(
+                            out=banks[kp][:, u, tt * P : (tt + 1) * P],
+                            in_=x_words[:, 256 * kp + u : 256 * (kp + 1) : 2],
+                            identity=ident[:],
+                        )
+            grouped = keep.tile([P, PASSES, 4 * BLOCK], BF16, name="xg%d" % blk, align_bytes=64)
+            for kp in range(PASSES):
+                dst = grouped[:, kp, :].bitcast(F32).rearrange("p (w u) -> p w u", u=2)
+                src = banks[kp][:].rearrange("p u w -> p w u")
+                if kp % 2 == 0:
+                    nc.vector.tensor_copy(out=dst, in_=src)
+                else:
+                    nc.scalar.copy(out=dst, in_=src)
+            codes = keep.tile([P, PASSES, BLOCK], U32, name="xc%d" % blk, align_bytes=64)
+            scales = keep.tile([P, PASSES, BLOCK], U8, name="xs%d" % blk, align_bytes=64)
+            nc.vector.quantize_mx(
+                out=codes[:].rearrange("p g w -> p (g w)").bitcast(FP8X4),
+                scales=scales[:].rearrange("p g w -> p (g w)"),
+                in_=grouped[:].rearrange("p g c -> p (g c)"),
+            )
+            x_codes.append(codes)
+            x_scales.append(scales)
+
+        quantise_x(0)
+
+        tables = []
+        for side in range(2):
+            table = keep.tile([P, TOKENS, 2], BF16, name="table%d" % side)
+            for blk in range(BLOCKS):
+                bank = psum.tile([P, 2, BLOCK], F32, name="bank")
+                for half in range(2):
+                    for tt in range(TILES_PER_BLOCK):
+                        nc.tensor.transpose(
+                            out=bank[:, half, tt * P : (tt + 1) * P],
+                            in_=table_src[:, blk * TILES_PER_BLOCK + tt, 2 * side + half, :],
+                            identity=ident[:],
+                        )
+                nc.scalar.copy(
+                    out=table[:, blk * BLOCK : (blk + 1) * BLOCK, :], in_=bank[:].rearrange("p h w -> p w h")
+                )
+            tables.append(table)
+
+        quantise_x(1)
+
+        rot_codes = []
+        rot_scales = []
+        for w in range(2):
+            rot_codes.append(keep.tile([P, GROUPS, TOKENS], U32, name="rc%d" % w, align_bytes=64))
+            rot_scales.append(keep.tile([P, GROUPS, TOKENS], U8, name="rs%d" % w, align_bytes=64))
+
+        def project_and_rotate(w, grp, blk):
+            tok = slice(blk * BLOCK, (blk + 1) * BLOCK)
+            products = []
+            for half in range(2):
+                bank = psum.tile([P, PAIRS, BLOCK], F32, name="bank")
+                for pair in range(PAIRS):
+                    first = half * (HIDDEN // 2) + (4 * grp + 2 * pair) * HALF
+                    for kp in range(PASSES):
+                        nc.tensor.matmul_mx(
+                            out=bank[:, pair, :],
+                            lhsT=w_sb[w][grp][:, kp, half, pair * P : (pair + 1) * P].bitcast(FP8X4),
+                            lhsT_scale=planes[w][4 * kp : P, first : first + P],
+                            rhs=x_codes[blk][:, kp, :].bitcast(FP8X4),
+                            rhs_scale=x_scales[blk][:, kp, :],
+                            start=(kp == 0),
+                            stop=(kp == PASSES - 1),
+                        )
+                product = work.tile([P, BLOCK, PAIRS, 2], F32, name="product%d" % half)
+                shape = [P, BLOCK, PAIRS, 2]
+                nc.vector.tensor_tensor(
+                    out=product[:],
+                    in0=bank[:].rearrange("p r w -> p w r").unsqueeze(3).to_broadcast(shape),
+                    in1=tables[half][:, tok, :].unsqueeze(2).to_broadcast(shape),
+                    op=MULT,
+                )
+                products.append(product)
+            rotated = work.tile([P, 4 * BLOCK], BF16, name="rotated", align_bytes=64)
+            nc.gpsimd.tensor_tensor(
+                out=rotated[:],
+                in0=products[0][:].rearrange("p w r h -> p (w r h)"),
+                in1=products[1][:].rearrange("p w r h -> p (w r h)"),
+                op=ADD,
+            )
+            return rotated
+
+        def quantise(w, grp, blk, rotated):
+            tok = slice(blk * BLOCK, (blk + 1) * BLOCK)
+            nc.vector.quantize_mx(
+                out=rot_codes[w][:, grp, tok].bitcast(FP8X4), scales=rot_scales[w][:, grp, tok], in_=rotated[:]
+            )
+
+        def score_pass(acc, t, grp):
+            rows = slice(t * P, (t + 1) * P)
+            nc.tensor.matmul_mx(
+                out=acc[:],
+                lhsT=rot_codes[1][:, grp, rows].bitcast(FP8X4),
+                lhsT_scale=rot_scales[1][:, grp, rows],
+                rhs=rot_codes[0][:, grp, :].bitcast(FP8X4),
+                rhs_scale=rot_scales[0][:, grp, :],
+                start=(grp == 0),
+                stop=(grp == GROUPS - 1),
+            )
+
+        def finish(acc, t):
+            result = work.tile([P, TOKENS], F32, name="result")
+            nc.vector.scalar_tensor_tensor(
+                out=result[:],
+                in0=acc[:],
+                scalar=1.0 / math.sqrt(CHUNK),
+                in1=mask_sb[:, t, :],
+                op0=MULT,
+                op1=ADD,
+            )
+            nc.sync.dma_start(out=out[0, t * P : (t + 1) * P, :], in_=result[:])
+
+        units = [(w, grp, blk) for w in range(2) for grp in range(GROUPS) for blk in range(BLOCKS)]
+        waiting = None
+        for unit in units:
+            rotated = project_and_rotate(*unit)
+            if waiting is not None:
+                quantise(*waiting)
+            waiting = unit + (rotated,)
+
+        accs = [psum.tile([P, TOKENS], F32, name="bank") for t in range(TOKEN_TILES)]
+        for grp in range(GROUPS - 1):
+            for t in range(TOKEN_TILES):
+                score_pass(accs[t], t, grp)
+        for t in range(TILES_PER_BLOCK):
+            score_pass(accs[t], t, GROUPS - 1)
+            finish(accs[t], t)
+        quantise(*waiting)
+        for t in range(TILES_PER_BLOCK, TOKEN_TILES):
+            score_pass(accs[t], t, GROUPS - 1)
+            finish(accs[t], t)

@@ -40,6 +40,7 @@ def tile_llamaattention_pa_kernel(
     with ExitStack() as ctx:
         keep = ctx.enter_context(tc.tile_pool(name="keep", bufs=1))
         work = ctx.enter_context(tc.tile_pool(name="work", bufs=3))
+        single = ctx.enter_context(tc.tile_pool(name="single", bufs=1))
         psum = ctx.enter_context(tc.psum_pool(name="psum", bufs=8))
         ctx.enter_context(tc.manual_schedule())
 
@@ -166,7 +167,7 @@ def tile_llamaattention_pa_kernel(
             rot_codes.append(keep.tile([P, GROUPS, TOKENS], U32, name="rc%d" % w, align_bytes=64))
             rot_scales.append(keep.tile([P, GROUPS, TOKENS], U8, name="rs%d" % w, align_bytes=64))
 
-        def project_and_rotate(w, grp, blk):
+        def project_and_multiply(w, grp, blk):
             tok = slice(blk * BLOCK, (blk + 1) * BLOCK)
             products = []
             for half in range(2):
@@ -192,19 +193,21 @@ def tile_llamaattention_pa_kernel(
                     op=MULT,
                 )
                 products.append(product)
-            rotated = work.tile([P, 4 * BLOCK], BF16, name="rotated", align_bytes=64)
+            return products
+
+        def add_products(rotated, blk, products):
             nc.gpsimd.tensor_tensor(
-                out=rotated[:],
+                out=rotated[:, blk, :],
                 in0=products[0][:].rearrange("p w r h -> p (w r h)"),
                 in1=products[1][:].rearrange("p w r h -> p (w r h)"),
                 op=ADD,
             )
-            return rotated
 
-        def quantise(w, grp, blk, rotated):
-            tok = slice(blk * BLOCK, (blk + 1) * BLOCK)
+        def quantise(w, grp, rotated):
             nc.vector.quantize_mx(
-                out=rot_codes[w][:, grp, tok].bitcast(FP8X4), scales=rot_scales[w][:, grp, tok], in_=rotated[:]
+                out=rot_codes[w][:, grp, :].bitcast(FP8X4),
+                scales=rot_scales[w][:, grp, :],
+                in_=rotated[:].rearrange("p b c -> p (b c)"),
             )
 
         def score_pass(acc, t, grp):
@@ -231,22 +234,22 @@ def tile_llamaattention_pa_kernel(
             )
             nc.sync.dma_start(out=out[0, t * P : (t + 1) * P, :], in_=result[:])
 
-        units = [(w, grp, blk) for w in range(2) for grp in range(GROUPS) for blk in range(BLOCKS)]
         waiting = None
-        for unit in units:
-            rotated = project_and_rotate(*unit)
-            if waiting is not None:
-                quantise(*waiting)
-            waiting = unit + (rotated,)
+        for w in range(2):
+            for grp in range(GROUPS):
+                products = project_and_multiply(w, grp, 0)
+                if waiting is not None:
+                    quantise(*waiting)
+                rotated = single.tile([P, BLOCKS, 4 * BLOCK], BF16, name="rotated", align_bytes=64)
+                add_products(rotated, 0, products)
+                add_products(rotated, 1, project_and_multiply(w, grp, 1))
+                waiting = (w, grp, rotated)
 
         accs = [psum.tile([P, TOKENS], F32, name="bank") for t in range(TOKEN_TILES)]
         for grp in range(GROUPS - 1):
             for t in range(TOKEN_TILES):
                 score_pass(accs[t], t, grp)
-        for t in range(TILES_PER_BLOCK):
-            score_pass(accs[t], t, GROUPS - 1)
-            finish(accs[t], t)
         quantise(*waiting)
-        for t in range(TILES_PER_BLOCK, TOKEN_TILES):
+        for t in range(TOKEN_TILES):
             score_pass(accs[t], t, GROUPS - 1)
             finish(accs[t], t)

@@ -27,6 +27,7 @@ BLOCKS = TOKENS // BLOCK
 TILES_PER_BLOCK = BLOCK // P
 GROUPS = PASSES
 PAIRS = 2
+GPSIMD_TOKENS = 160
 
 FLOPS = 2 * (2 * TOKENS * HIDDEN * HIDDEN) + 2 * TOKENS * TOKENS * HIDDEN
 
@@ -52,6 +53,12 @@ def tile_llamaattention_pa_kernel(
         nc.scalar.dma_start(out=cos_sb[:], in_=cos.rearrange("(t p) f -> p t f", p=P))
         nc.scalar.dma_start(out=sin_sb[:], in_=sin.rearrange("(t p) f -> p t f", p=P))
 
+        x_sb = []
+        for t in range(TOKEN_TILES):
+            x_t = keep.tile([P, HIDDEN], BF16, name="x%d" % t)
+            nc.sync.dma_start(out=x_t[:], in_=hidden_states[0, t * P : (t + 1) * P, :])
+            x_sb.append(x_t)
+
         staged = []
         for w in range(2):
             stage = keep.tile([P, HIDDEN], U8, name="stage%d" % w, align_bytes=64)
@@ -62,12 +69,6 @@ def tile_llamaattention_pa_kernel(
                     in_=weights_dram[w][1][:, 4 * quad : 4 * quad + 4, :].bitcast(I32),
                 )
             staged.append(stage)
-
-        x_sb = []
-        for t in range(TOKEN_TILES):
-            x_t = keep.tile([P, HIDDEN], BF16, name="x%d" % t)
-            nc.sync.dma_start(out=x_t[:], in_=hidden_states[0, t * P : (t + 1) * P, :])
-            x_sb.append(x_t)
 
         w_sb = []
         for w in range(2):
@@ -195,15 +196,17 @@ def tile_llamaattention_pa_kernel(
                 products.append(product)
             return products
 
-        def add_products(rotated, blk, products):
-            nc.gpsimd.tensor_tensor(
-                out=rotated[:, blk, :],
-                in0=products[0][:].rearrange("p w r h -> p (w r h)"),
-                in1=products[1][:].rearrange("p w r h -> p (w r h)"),
+        def add_products(engine, rotated, blk, products, tokens):
+            cols = slice(4 * tokens[0], 4 * tokens[1])
+            engine.tensor_tensor(
+                out=rotated[:, blk, cols],
+                in0=products[0][:].rearrange("p w r h -> p (w r h)")[:, cols],
+                in1=products[1][:].rearrange("p w r h -> p (w r h)")[:, cols],
                 op=ADD,
             )
 
-        def quantise(w, grp, rotated):
+        def quantise(w, grp, rotated, products, split):
+            add_products(nc.vector, rotated, 1, products, (split, BLOCK))
             nc.vector.quantize_mx(
                 out=rot_codes[w][:, grp, :].bitcast(FP8X4),
                 scales=rot_scales[w][:, grp, :],
@@ -241,9 +244,12 @@ def tile_llamaattention_pa_kernel(
                 if waiting is not None:
                     quantise(*waiting)
                 rotated = single.tile([P, BLOCKS, 4 * BLOCK], BF16, name="rotated", align_bytes=64)
-                add_products(rotated, 0, products)
-                add_products(rotated, 1, project_and_multiply(w, grp, 1))
-                waiting = (w, grp, rotated)
+                add_products(nc.gpsimd, rotated, 0, products, (0, BLOCK))
+                products = project_and_multiply(w, grp, 1)
+                split = 0 if (w, grp) == (1, GROUPS - 1) else GPSIMD_TOKENS
+                if split > 0:
+                    add_products(nc.gpsimd, rotated, 1, products, (0, split))
+                waiting = (w, grp, rotated, products, split)
 
         accs = [psum.tile([P, TOKENS], F32, name="bank") for t in range(TOKEN_TILES)]
         for grp in range(GROUPS - 1):

@@ -27,7 +27,6 @@ BLOCKS = TOKENS // BLOCK
 TILES_PER_BLOCK = BLOCK // P
 GROUPS = PASSES
 PAIRS = 2
-GPSIMD_TOKENS = 160
 
 FLOPS = 2 * (2 * TOKENS * HIDDEN * HIDDEN) + 2 * TOKENS * TOKENS * HIDDEN
 
@@ -41,7 +40,7 @@ def tile_llamaattention_pa_kernel(
     with ExitStack() as ctx:
         keep = ctx.enter_context(tc.tile_pool(name="keep", bufs=1))
         work = ctx.enter_context(tc.tile_pool(name="work", bufs=3))
-        single = ctx.enter_context(tc.tile_pool(name="single", bufs=1))
+        double = ctx.enter_context(tc.tile_pool(name="double", bufs=2))
         psum = ctx.enter_context(tc.psum_pool(name="psum", bufs=8))
         ctx.enter_context(tc.manual_schedule())
 
@@ -196,17 +195,15 @@ def tile_llamaattention_pa_kernel(
                 products.append(product)
             return products
 
-        def add_products(engine, rotated, blk, products, tokens):
-            cols = slice(4 * tokens[0], 4 * tokens[1])
+        def add_products(engine, rotated, blk, products):
             engine.tensor_tensor(
-                out=rotated[:, blk, cols],
-                in0=products[0][:].rearrange("p w r h -> p (w r h)")[:, cols],
-                in1=products[1][:].rearrange("p w r h -> p (w r h)")[:, cols],
+                out=rotated[:, blk, :],
+                in0=products[0][:].rearrange("p w r h -> p (w r h)"),
+                in1=products[1][:].rearrange("p w r h -> p (w r h)"),
                 op=ADD,
             )
 
-        def quantise(w, grp, rotated, products, split):
-            add_products(nc.vector, rotated, 1, products, (split, BLOCK))
+        def quantise(w, grp, rotated):
             nc.vector.quantize_mx(
                 out=rot_codes[w][:, grp, :].bitcast(FP8X4),
                 scales=rot_scales[w][:, grp, :],
@@ -240,16 +237,14 @@ def tile_llamaattention_pa_kernel(
         waiting = None
         for w in range(2):
             for grp in range(GROUPS):
-                products = project_and_multiply(w, grp, 0)
+                rotated = double.tile([P, BLOCKS, 4 * BLOCK], BF16, name="rotated", align_bytes=64)
+                add_products(nc.gpsimd, rotated, 0, project_and_multiply(w, grp, 0))
+                products = project_and_multiply(w, grp, 1)
                 if waiting is not None:
                     quantise(*waiting)
-                rotated = single.tile([P, BLOCKS, 4 * BLOCK], BF16, name="rotated", align_bytes=64)
-                add_products(nc.gpsimd, rotated, 0, products, (0, BLOCK))
-                products = project_and_multiply(w, grp, 1)
-                split = 0 if (w, grp) == (1, GROUPS - 1) else GPSIMD_TOKENS
-                if split > 0:
-                    add_products(nc.gpsimd, rotated, 1, products, (0, split))
-                waiting = (w, grp, rotated, products, split)
+                last = (w, grp) == (1, GROUPS - 1)
+                add_products(nc.vector if last else nc.gpsimd, rotated, 1, products)
+                waiting = (w, grp, rotated)
 
         accs = [psum.tile([P, TOKENS], F32, name="bank") for t in range(TOKEN_TILES)]
         for grp in range(GROUPS - 1):

@@ -41,6 +41,7 @@ def tile_llamaattention_pa_kernel(
         keep = ctx.enter_context(tc.tile_pool(name="keep", bufs=1))
         work = ctx.enter_context(tc.tile_pool(name="work", bufs=3))
         double = ctx.enter_context(tc.tile_pool(name="double", bufs=2))
+        results = ctx.enter_context(tc.tile_pool(name="results", bufs=TOKEN_TILES))
         psum = ctx.enter_context(tc.psum_pool(name="psum", bufs=8))
         ctx.enter_context(tc.manual_schedule())
 
@@ -99,15 +100,6 @@ def tile_llamaattention_pa_kernel(
                 scalar1=(-1.0 if k == 2 else 1.0),
             )
 
-        planes = []
-        for w in range(2):
-            plane = keep.tile([P, HIDDEN], U8, name="plane%d" % w, align_bytes=64)
-            nc.vector.tensor_copy(
-                out=plane[:].bitcast(I32).rearrange("p (h c i) -> p h c i", h=2, c=N_CHUNKS),
-                in_=staged[w][:].bitcast(I32).rearrange("p (c h i) -> p h c i", h=2, c=N_CHUNKS),
-            )
-            planes.append(plane)
-
         x_codes = []
         x_scales = []
 
@@ -158,6 +150,15 @@ def tile_llamaattention_pa_kernel(
                     out=table[:, blk * BLOCK : (blk + 1) * BLOCK, :], in_=bank[:].rearrange("p h w -> p w h")
                 )
             tables.append(table)
+
+        planes = []
+        for w in range(2):
+            plane = keep.tile([P, HIDDEN], U8, name="plane%d" % w, align_bytes=64)
+            nc.vector.tensor_copy(
+                out=plane[:].bitcast(I32).rearrange("p (h c i) -> p h c i", h=2, c=N_CHUNKS),
+                in_=staged[w][:].bitcast(I32).rearrange("p (c h i) -> p h c i", h=2, c=N_CHUNKS),
+            )
+            planes.append(plane)
 
         quantise_x(1)
 
@@ -223,7 +224,7 @@ def tile_llamaattention_pa_kernel(
             )
 
         def finish(acc, t):
-            result = work.tile([P, TOKENS], F32, name="result")
+            result = results.tile([P, TOKENS], F32, name="result")
             nc.vector.scalar_tensor_tensor(
                 out=result[:],
                 in0=acc[:],

@@ -53,39 +53,49 @@ def tile_llamaattention_pa_kernel(
         nc.scalar.dma_start(out=cos_sb[:], in_=cos.rearrange("(t p) f -> p t f", p=P))
         nc.scalar.dma_start(out=sin_sb[:], in_=sin.rearrange("(t p) f -> p t f", p=P))
 
-        x_sb = []
-        for t in range(TOKEN_TILES):
-            x_t = keep.tile([P, HIDDEN], BF16, name="x%d" % t)
-            nc.sync.dma_start(out=x_t[:], in_=hidden_states[0, t * P : (t + 1) * P, :])
-            x_sb.append(x_t)
-
         staged = []
         for w in range(2):
             stage = keep.tile([P, HIDDEN], U8, name="stage%d" % w, align_bytes=64)
             nc.vector.memset(stage[:].bitcast(I32), 0)
-            for quad in range(4):
-                nc.sync.dma_start(
-                    out=stage[32 * quad : 32 * quad + 16, :].bitcast(I32),
-                    in_=weights_dram[w][1][:, 4 * quad : 4 * quad + 4, :].bitcast(I32),
-                )
             staged.append(stage)
 
-        w_sb = []
-        for w in range(2):
-            per_group = []
-            for grp in range(GROUPS):
-                w_g = keep.tile([P, PASSES, 2, 4 * HALF], U32, name="w%d_%d" % (w, grp), align_bytes=64)
-                for half in range(2):
-                    for kp in range(PASSES):
-                        words = weights_dram[w][0][kp].rearrange("p n t -> p (n t)").bitcast(I32)
-                        nc.sync.dma_start(
-                            out=w_g[:, kp, half, :].bitcast(I32).rearrange("p (c i) -> p c i", i=HALF),
-                            in_=words.rearrange("p (c h i) -> p c h i", h=2, i=HALF)[
-                                :, 4 * grp : 4 * grp + 4, half, :
-                            ],
-                        )
-                per_group.append(w_g)
-            w_sb.append(per_group)
+        x_sb = []
+
+        def load_x(t):
+            x_t = keep.tile([P, HIDDEN], BF16, name="x%d" % t)
+            nc.sync.dma_start(out=x_t[:], in_=hidden_states[0, t * P : (t + 1) * P, :])
+            x_sb.append(x_t)
+
+        def load_scales(w):
+            for quad in range(4):
+                nc.sync.dma_start(
+                    out=staged[w][32 * quad : 32 * quad + 16, :].bitcast(I32),
+                    in_=weights_dram[w][1][:, 4 * quad : 4 * quad + 4, :].bitcast(I32),
+                )
+
+        w_sb = [[], []]
+
+        def load_weights(w, grp):
+            w_g = keep.tile([P, PASSES, 2, 4 * HALF], U32, name="w%d_%d" % (w, grp), align_bytes=64)
+            for half in range(2):
+                for kp in range(PASSES):
+                    words = weights_dram[w][0][kp].rearrange("p n t -> p (n t)").bitcast(I32)
+                    nc.sync.dma_start(
+                        out=w_g[:, kp, half, :].bitcast(I32).rearrange("p (c i) -> p c i", i=HALF),
+                        in_=words.rearrange("p (c h i) -> p c h i", h=2, i=HALF)[:, 4 * grp : 4 * grp + 4, half, :],
+                    )
+            w_sb[w].append(w_g)
+
+        for t in range(TOKEN_TILES):
+            load_x(t)
+        load_scales(0)
+        for grp in range(2):
+            load_weights(0, grp)
+        load_scales(1)
+        for grp in range(2, GROUPS):
+            load_weights(0, grp)
+        for grp in range(GROUPS):
+            load_weights(1, grp)
 
         mask_sb = keep.tile([P, TOKEN_TILES, TOKENS], BF16)
         nc.sync.dma_start(out=mask_sb[:], in_=attention_mask[0].rearrange("(t p) s -> p t s", p=P))
@@ -94,16 +104,20 @@ def tile_llamaattention_pa_kernel(
         twice = [P, TOKEN_TILES, 2, HALF]
         sources = (cos_sb[:, :, 0:HALF], sin_sb[:, :, HALF:CHUNK], sin_sb[:, :, 0:HALF], cos_sb[:, :, HALF:CHUNK])
         for k in range(4):
-            nc.vector.tensor_scalar_mul(
+            nc.gpsimd.tensor_scalar(
                 out=table_src[:, :, k, :].rearrange("p t (d i) -> p t d i", d=2),
                 in0=sources[k].unsqueeze(2).to_broadcast(twice),
                 scalar1=(-1.0 if k == 2 else 1.0),
+                scalar2=0.0,
+                op0=MULT,
+                op1=ADD,
             )
 
+        x_grouped = []
         x_codes = []
         x_scales = []
 
-        def quantise_x(blk):
+        def transpose_x(blk):
             banks = [psum.tile([P, 2, BLOCK], F32, name="bank") for kp in range(PASSES)]
             for tt in range(TILES_PER_BLOCK):
                 x_words = x_sb[blk * TILES_PER_BLOCK + tt][:].bitcast(F32)
@@ -122,22 +136,25 @@ def tile_llamaattention_pa_kernel(
                     nc.vector.tensor_copy(out=dst, in_=src)
                 else:
                     nc.scalar.copy(out=dst, in_=src)
+            x_grouped.append(grouped)
+
+        def quantise_x(blk):
+            grouped = x_grouped[blk]
             codes = keep.tile([P, PASSES, BLOCK], U32, name="xc%d" % blk, align_bytes=64)
             scales = keep.tile([P, PASSES, BLOCK], U8, name="xs%d" % blk, align_bytes=64)
-            nc.vector.quantize_mx(
-                out=codes[:].rearrange("p g w -> p (g w)").bitcast(FP8X4),
-                scales=scales[:].rearrange("p g w -> p (g w)"),
-                in_=grouped[:].rearrange("p g c -> p (g c)"),
-            )
+            for first in range(0, PASSES, 2):
+                nc.vector.quantize_mx(
+                    out=codes[:, first : first + 2, :].rearrange("p g w -> p (g w)").bitcast(FP8X4),
+                    scales=scales[:, first : first + 2, :].rearrange("p g w -> p (g w)"),
+                    in_=grouped[:, first : first + 2, :].rearrange("p g c -> p (g c)"),
+                )
             x_codes.append(codes)
             x_scales.append(scales)
 
-        quantise_x(0)
+        tables = [keep.tile([P, TOKENS, 2], BF16, name="table%d" % side) for side in range(2)]
 
-        tables = []
-        for side in range(2):
-            table = keep.tile([P, TOKENS, 2], BF16, name="table%d" % side)
-            for blk in range(BLOCKS):
+        def make_tables(blk):
+            for side in range(2):
                 bank = psum.tile([P, 2, BLOCK], F32, name="bank")
                 for half in range(2):
                     for tt in range(TILES_PER_BLOCK):
@@ -147,12 +164,12 @@ def tile_llamaattention_pa_kernel(
                             identity=ident[:],
                         )
                 nc.scalar.copy(
-                    out=table[:, blk * BLOCK : (blk + 1) * BLOCK, :], in_=bank[:].rearrange("p h w -> p w h")
+                    out=tables[side][:, blk * BLOCK : (blk + 1) * BLOCK, :], in_=bank[:].rearrange("p h w -> p w h")
                 )
-            tables.append(table)
 
         planes = []
-        for w in range(2):
+
+        def arrange_plane(w):
             plane = keep.tile([P, HIDDEN], U8, name="plane%d" % w, align_bytes=64)
             nc.vector.tensor_copy(
                 out=plane[:].bitcast(I32).rearrange("p (h c i) -> p h c i", h=2, c=N_CHUNKS),
@@ -160,7 +177,12 @@ def tile_llamaattention_pa_kernel(
             )
             planes.append(plane)
 
+        transpose_x(0)
+        quantise_x(0)
+        transpose_x(1)
+        arrange_plane(0)
         quantise_x(1)
+        make_tables(0)
 
         rot_codes = []
         rot_scales = []
@@ -196,19 +218,19 @@ def tile_llamaattention_pa_kernel(
                 products.append(product)
             return products
 
-        def add_products(engine, rotated, blk, products):
+        def add_products(engine, rotated, blk, products, first=0, count=BLOCK):
             engine.tensor_tensor(
-                out=rotated[:, blk, :],
-                in0=products[0][:].rearrange("p w r h -> p (w r h)"),
-                in1=products[1][:].rearrange("p w r h -> p (w r h)"),
+                out=rotated[:, blk, 4 * first : 4 * (first + count)],
+                in0=products[0][:, first : first + count].rearrange("p w r h -> p (w r h)"),
+                in1=products[1][:, first : first + count].rearrange("p w r h -> p (w r h)"),
                 op=ADD,
             )
 
-        def quantise(w, grp, rotated):
+        def quantise(w, grp, rotated, first=0, count=TOKENS):
             nc.vector.quantize_mx(
-                out=rot_codes[w][:, grp, :].bitcast(FP8X4),
-                scales=rot_scales[w][:, grp, :],
-                in_=rotated[:].rearrange("p b c -> p (b c)"),
+                out=rot_codes[w][:, grp, first : first + count].bitcast(FP8X4),
+                scales=rot_scales[w][:, grp, first : first + count],
+                in_=rotated[:].rearrange("p b c -> p (b c)")[:, 4 * first : 4 * (first + count)],
             )
 
         def score_pass(acc, t, grp):
@@ -240,18 +262,30 @@ def tile_llamaattention_pa_kernel(
             for grp in range(GROUPS):
                 rotated = double.tile([P, BLOCKS, 4 * BLOCK], BF16, name="rotated", align_bytes=64)
                 add_products(nc.gpsimd, rotated, 0, project_and_multiply(w, grp, 0))
-                products = project_and_multiply(w, grp, 1)
-                if waiting is not None:
-                    quantise(*waiting)
+                if (w, grp) == (0, 0):
+                    make_tables(1)
+                if (w, grp) == (0, 1):
+                    arrange_plane(1)
                 last = (w, grp) == (1, GROUPS - 1)
-                add_products(nc.vector if last else nc.gpsimd, rotated, 1, products)
-                waiting = (w, grp, rotated)
+                if last:
+                    quantise(*waiting)
+                products = project_and_multiply(w, grp, 1)
+                if not last:
+                    if waiting is not None:
+                        quantise(*waiting)
+                    add_products(nc.gpsimd, rotated, 1, products)
+                    waiting = (w, grp, rotated)
 
         accs = [psum.tile([P, TOKENS], F32, name="bank") for t in range(TOKEN_TILES)]
         for grp in range(GROUPS - 1):
             for t in range(TOKEN_TILES):
                 score_pass(accs[t], t, grp)
-        quantise(*waiting)
+        quantise(1, GROUPS - 1, rotated, 0, BLOCK)
+        for t in (2, 3):
+            add_products(nc.vector, rotated, 1, products, (t - 2) * P, P)
+        for t in (2, 3):
+            quantise(1, GROUPS - 1, rotated, t * P, P)
         for t in range(TOKEN_TILES):
             score_pass(accs[t], t, GROUPS - 1)
+        for t in range(TOKEN_TILES):
             finish(accs[t], t)

@@ -48,10 +48,16 @@ def tile_llamaattention_pa_kernel(
         ident = keep.tile([P, P], F32)
         make_identity(nc, ident[:])
 
-        cos_sb = keep.tile([P, TOKEN_TILES, CHUNK], BF16)
-        sin_sb = keep.tile([P, TOKEN_TILES, CHUNK], BF16)
-        nc.scalar.dma_start(out=cos_sb[:], in_=cos.rearrange("(t p) f -> p t f", p=P))
-        nc.scalar.dma_start(out=sin_sb[:], in_=sin.rearrange("(t p) f -> p t f", p=P))
+        factors = keep.tile([P, TOKEN_TILES, 8 * HALF], BF16)
+        nc.scalar.dma_start(out=factors[:, :, 2 * HALF : 4 * HALF], in_=cos.rearrange("(t p) f -> p t f", p=P))
+        nc.scalar.dma_start(out=factors[:, :, 4 * HALF : 6 * HALF], in_=sin.rearrange("(t p) f -> p t f", p=P))
+
+        zeros = keep.tile([P, TOKENS], BF16)
+        nc.vector.memset(zeros[:], 0.0)
+
+        def keep_warm(bank, count):
+            for i in range(count):
+                nc.tensor.matmul(bank[:], lhsT=zeros[:, 0:P], rhs=zeros[:], start=True, stop=True)
 
         staged = []
         for w in range(2):
@@ -100,24 +106,21 @@ def tile_llamaattention_pa_kernel(
         mask_sb = keep.tile([P, TOKEN_TILES, TOKENS], BF16)
         nc.sync.dma_start(out=mask_sb[:], in_=attention_mask[0].rearrange("(t p) s -> p t s", p=P))
 
-        table_src = keep.tile([P, TOKEN_TILES, 4, CHUNK], F32)
-        twice = [P, TOKEN_TILES, 2, HALF]
-        sources = (cos_sb[:, :, 0:HALF], sin_sb[:, :, HALF:CHUNK], sin_sb[:, :, 0:HALF], cos_sb[:, :, HALF:CHUNK])
-        for k in range(4):
-            nc.gpsimd.tensor_scalar(
-                out=table_src[:, :, k, :].rearrange("p t (d i) -> p t d i", d=2),
-                in0=sources[k].unsqueeze(2).to_broadcast(twice),
-                scalar1=(-1.0 if k == 2 else 1.0),
-                scalar2=0.0,
-                op0=MULT,
-                op1=ADD,
-            )
+        nc.vector.tensor_scalar_mul(
+            out=factors[:, :, 0:HALF], in0=factors[:, :, 4 * HALF : 5 * HALF], scalar1=-1.0
+        )
+        table_src = keep.tile([P, TOKEN_TILES, 2, 2, HALF, 2], BF16)
+        for side in range(2):
+            first = 2 * HALF * (1 - side)
+            pairs = factors[:, :, first : first + 6 * HALF].rearrange("p t (h s) -> p t s h", h=2)[:, :, 0:HALF, :]
+            for copy in range(2):
+                nc.vector.tensor_copy(out=table_src[:, :, side, copy], in_=pairs)
 
         x_grouped = []
         x_codes = []
         x_scales = []
 
-        def transpose_x(blk):
+        def transpose_x(blk, idle_bank):
             banks = [psum.tile([P, 2, BLOCK], F32, name="bank") for kp in range(PASSES)]
             for tt in range(TILES_PER_BLOCK):
                 x_words = x_sb[blk * TILES_PER_BLOCK + tt][:].bitcast(F32)
@@ -128,6 +131,8 @@ def tile_llamaattention_pa_kernel(
                             in_=x_words[:, 256 * kp + u : 256 * (kp + 1) : 2],
                             identity=ident[:],
                         )
+                    if kp % 2 == 1:
+                        keep_warm(idle_bank, 1)
             grouped = keep.tile([P, PASSES, 4 * BLOCK], BF16, name="xg%d" % blk, align_bytes=64)
             for kp in range(PASSES):
                 dst = grouped[:, kp, :].bitcast(F32).rearrange("p (w u) -> p w u", u=2)
@@ -151,21 +156,18 @@ def tile_llamaattention_pa_kernel(
             x_codes.append(codes)
             x_scales.append(scales)
 
-        tables = [keep.tile([P, TOKENS, 2], BF16, name="table%d" % side) for side in range(2)]
+        tables = [keep.tile([P, TOKENS, 2], BF16, name="table%d" % side, align_bytes=64) for side in range(2)]
 
-        def make_tables(blk):
+        def make_tables():
             for side in range(2):
-                bank = psum.tile([P, 2, BLOCK], F32, name="bank")
-                for half in range(2):
-                    for tt in range(TILES_PER_BLOCK):
-                        nc.tensor.transpose(
-                            out=bank[:, half, tt * P : (tt + 1) * P],
-                            in_=table_src[:, blk * TILES_PER_BLOCK + tt, 2 * side + half, :],
-                            identity=ident[:],
-                        )
-                nc.scalar.copy(
-                    out=tables[side][:, blk * BLOCK : (blk + 1) * BLOCK, :], in_=bank[:].rearrange("p h w -> p w h")
-                )
+                bank = psum.tile([P, TOKENS], F32, name="bank")
+                for t in range(TOKEN_TILES):
+                    nc.tensor.transpose(
+                        out=bank[:, t * P : (t + 1) * P],
+                        in_=table_src[:, t, side].rearrange("p d i h -> p (d i h)").bitcast(F32),
+                        identity=ident[:],
+                    )
+                nc.scalar.copy(out=tables[side][:].rearrange("p w h -> p (w h)").bitcast(F32), in_=bank[:])
 
         planes = []
 
@@ -177,12 +179,17 @@ def tile_llamaattention_pa_kernel(
             )
             planes.append(plane)
 
-        transpose_x(0)
+        idle_bank = psum.tile([P, TOKENS], F32, name="bank")
+        keep_warm(idle_bank, 6)
+        transpose_x(0, idle_bank)
         quantise_x(0)
-        transpose_x(1)
+        make_tables()
+        idle_bank = psum.tile([P, TOKENS], F32, name="bank")
+        keep_warm(idle_bank, 2)
+        transpose_x(1, idle_bank)
+        keep_warm(idle_bank, 2)
         arrange_plane(0)
         quantise_x(1)
-        make_tables(0)
 
         rot_codes = []
         rot_scales = []
@@ -262,8 +269,6 @@ def tile_llamaattention_pa_kernel(
             for grp in range(GROUPS):
                 rotated = double.tile([P, BLOCKS, 4 * BLOCK], BF16, name="rotated", align_bytes=64)
                 add_products(nc.gpsimd, rotated, 0, project_and_multiply(w, grp, 0))
-                if (w, grp) == (0, 0):
-                    make_tables(1)
                 if (w, grp) == (0, 1):
                     arrange_plane(1)
                 last = (w, grp) == (1, GROUPS - 1)

@@ -79,18 +79,37 @@ def tile_llamaattention_pa_kernel(
                     in_=weights_dram[w][1][:, 4 * quad : 4 * quad + 4, :].bitcast(I32),
                 )
 
-        w_sb = [[], []]
+        inner = [keep.tile([P, PASSES, HIDDEN // 2], U32, name="inner%d" % w, align_bytes=64) for w in range(2)]
+        outer = [keep.tile([P, PASSES, HIDDEN // 2], U32, name="outer%d" % w, align_bytes=64) for w in range(2)]
+
+        def load_runs(w, kp, tile, to, source, runs):
+            words = weights_dram[w][0][kp].rearrange("p n t -> p (n t)").bitcast(I32)
+            stop = source + (runs - 1) * 2 * CHUNK + CHUNK
+            if runs > 1:
+                in_ = words[:, source - HALF : source - HALF + runs * 2 * CHUNK]
+                in_ = in_.rearrange("p (r s) -> p r s", r=runs)[:, :, HALF : HALF + CHUNK]
+            else:
+                in_ = words[:, source:stop].rearrange("p (r s) -> p r s", r=1)
+            nc.sync.dma_start(
+                out=tile[:, kp, to : to + runs * CHUNK].bitcast(I32).rearrange("p (r s) -> p r s", r=runs), in_=in_
+            )
+
+        def load_end(w, to, source):
+            words = weights_dram[w][0].rearrange("g p n t -> p g (n t)").bitcast(I32)
+            nc.sync.dma_start(
+                out=outer[w][:, :, to : to + HALF].bitcast(I32), in_=words[:, :, source : source + HALF]
+            )
 
         def load_weights(w, grp):
-            w_g = keep.tile([P, PASSES, 2, 4 * HALF], U32, name="w%d_%d" % (w, grp), align_bytes=64)
-            for half in range(2):
-                for kp in range(PASSES):
-                    words = weights_dram[w][0][kp].rearrange("p n t -> p (n t)").bitcast(I32)
-                    nc.sync.dma_start(
-                        out=w_g[:, kp, half, :].bitcast(I32).rearrange("p (c i) -> p c i", i=HALF),
-                        in_=words.rearrange("p (c h i) -> p c h i", h=2, i=HALF)[:, 4 * grp : 4 * grp + 4, half, :],
-                    )
-            w_sb[w].append(w_g)
+            for kp in range(PASSES):
+                load_runs(w, kp, inner[w], 2 * CHUNK * grp, 4 * CHUNK * grp + HALF, 2)
+            if grp == 0:
+                load_end(w, 0, 0)
+            last = grp == GROUPS - 1
+            for kp in range(PASSES):
+                load_runs(w, kp, outer[w], 2 * CHUNK * grp + HALF, 4 * CHUNK * grp + 3 * HALF, 1 if last else 2)
+            if last:
+                load_end(w, HIDDEN // 2 - HALF, HIDDEN - HALF)
 
         for t in range(TOKEN_TILES):
             load_x(t)
@@ -113,8 +132,8 @@ def tile_llamaattention_pa_kernel(
         for side in range(2):
             first = 2 * HALF * (1 - side)
             pairs = factors[:, :, first : first + 6 * HALF].rearrange("p t (h s) -> p t s h", h=2)[:, :, 0:HALF, :]
-            for copy in range(2):
-                nc.vector.tensor_copy(out=table_src[:, :, side, copy], in_=pairs)
+            for table in range(2):
+                nc.vector.tensor_copy(out=table_src[:, :, table, 1 - side if table == 0 else side], in_=pairs)
 
         x_grouped = []
         x_codes = []
@@ -169,15 +188,19 @@ def tile_llamaattention_pa_kernel(
                     )
                 nc.scalar.copy(out=tables[side][:].rearrange("p w h -> p (w h)").bitcast(F32), in_=bank[:])
 
-        planes = []
+        outer_scales = []
 
         def arrange_plane(w):
-            plane = keep.tile([P, HIDDEN], U8, name="plane%d" % w, align_bytes=64)
+            plane = keep.tile([P, HIDDEN // 2], U8, name="plane%d" % w, align_bytes=64)
+            to = plane[:].bitcast(I32).rearrange("p (c i) -> p c i", i=HALF // 4)
+            source = staged[w][:].bitcast(I32).rearrange("p (c i) -> p c i", i=HALF // 4)
+            runs = N_CHUNKS // 2 - 1
             nc.vector.tensor_copy(
-                out=plane[:].bitcast(I32).rearrange("p (h c i) -> p h c i", h=2, c=N_CHUNKS),
-                in_=staged[w][:].bitcast(I32).rearrange("p (c h i) -> p h c i", h=2, c=N_CHUNKS),
+                out=to[:, 1 : 1 + 2 * runs].rearrange("p (r c) i -> p r (c i)", c=2),
+                in_=source[:, 2 : 2 + 4 * runs].rearrange("p (r c) i -> p r (c i)", c=4)[:, :, HALF // 4 : 3 * (HALF // 4)],
             )
-            planes.append(plane)
+            nc.vector.tensor_copy(out=to[:, :: N_CHUNKS - 1], in_=source[:, :: 2 * N_CHUNKS - 1])
+            outer_scales.append(plane)
 
         idle_bank = psum.tile([P, TOKENS], F32, name="bank")
         keep_warm(idle_bank, 6)
@@ -203,12 +226,16 @@ def tile_llamaattention_pa_kernel(
             for half in range(2):
                 bank = psum.tile([P, PAIRS, BLOCK], F32, name="bank")
                 for pair in range(PAIRS):
-                    first = half * (HIDDEN // 2) + (4 * grp + 2 * pair) * HALF
+                    first = (PAIRS * grp + pair) * CHUNK
+                    if half == 0:
+                        weights, scales, first_scale = inner[w], staged[w], 2 * first + HALF
+                    else:
+                        weights, scales, first_scale = outer[w], outer_scales[w], first
                     for kp in range(PASSES):
                         nc.tensor.matmul_mx(
                             out=bank[:, pair, :],
-                            lhsT=w_sb[w][grp][:, kp, half, pair * P : (pair + 1) * P].bitcast(FP8X4),
-                            lhsT_scale=planes[w][4 * kp : P, first : first + P],
+                            lhsT=weights[:, kp, first : first + P].bitcast(FP8X4),
+                            lhsT_scale=scales[4 * kp : P, first_scale : first_scale + P],
                             rhs=x_codes[blk][:, kp, :].bitcast(FP8X4),
                             rhs_scale=x_scales[blk][:, kp, :],
                             start=(kp == 0),

@@ -49,8 +49,8 @@ def tile_llamaattention_pa_kernel(
         make_identity(nc, ident[:])
 
         factors = keep.tile([P, TOKEN_TILES, 8 * HALF], BF16)
-        nc.scalar.dma_start(out=factors[:, :, 2 * HALF : 4 * HALF], in_=cos.rearrange("(t p) f -> p t f", p=P))
-        nc.scalar.dma_start(out=factors[:, :, 4 * HALF : 6 * HALF], in_=sin.rearrange("(t p) f -> p t f", p=P))
+        nc.sync.dma_start(out=factors[:, :, 2 * HALF : 4 * HALF], in_=cos.rearrange("(t p) f -> p t f", p=P))
+        nc.sync.dma_start(out=factors[:, :, 4 * HALF : 6 * HALF], in_=sin.rearrange("(t p) f -> p t f", p=P))
 
         zeros = keep.tile([P, TOKENS], BF16)
         nc.vector.memset(zeros[:], 0.0)
@@ -139,9 +139,11 @@ def tile_llamaattention_pa_kernel(
         x_codes = []
         x_scales = []
 
-        def transpose_x(blk, idle_bank):
+        def transpose_x(blk, idle_bank, vector_copies):
             banks = [psum.tile([P, 2, BLOCK], F32, name="bank") for kp in range(PASSES)]
             for tt in range(TILES_PER_BLOCK):
+                if tt > 0:
+                    keep_warm(idle_bank, TILES_PER_BLOCK - blk)
                 x_words = x_sb[blk * TILES_PER_BLOCK + tt][:].bitcast(F32)
                 for kp in range(PASSES):
                     for u in range(2):
@@ -150,30 +152,27 @@ def tile_llamaattention_pa_kernel(
                             in_=x_words[:, 256 * kp + u : 256 * (kp + 1) : 2],
                             identity=ident[:],
                         )
-                    if kp % 2 == 1:
-                        keep_warm(idle_bank, 1)
             grouped = keep.tile([P, PASSES, 4 * BLOCK], BF16, name="xg%d" % blk, align_bytes=64)
             for kp in range(PASSES):
                 dst = grouped[:, kp, :].bitcast(F32).rearrange("p (w u) -> p w u", u=2)
                 src = banks[kp][:].rearrange("p u w -> p w u")
-                if kp % 2 == 0:
+                if kp in vector_copies:
                     nc.vector.tensor_copy(out=dst, in_=src)
                 else:
                     nc.scalar.copy(out=dst, in_=src)
             x_grouped.append(grouped)
 
-        def quantise_x(blk):
-            grouped = x_grouped[blk]
-            codes = keep.tile([P, PASSES, BLOCK], U32, name="xc%d" % blk, align_bytes=64)
-            scales = keep.tile([P, PASSES, BLOCK], U8, name="xs%d" % blk, align_bytes=64)
-            for first in range(0, PASSES, 2):
-                nc.vector.quantize_mx(
-                    out=codes[:, first : first + 2, :].rearrange("p g w -> p (g w)").bitcast(FP8X4),
-                    scales=scales[:, first : first + 2, :].rearrange("p g w -> p (g w)"),
-                    in_=grouped[:, first : first + 2, :].rearrange("p g c -> p (g c)"),
-                )
-            x_codes.append(codes)
-            x_scales.append(scales)
+        for blk in range(BLOCKS):
+            x_codes.append(keep.tile([P, PASSES, BLOCK], U32, name="xc%d" % blk, align_bytes=64))
+            x_scales.append(keep.tile([P, PASSES, BLOCK], U8, name="xs%d" % blk, align_bytes=64))
+
+        def quantise_x(blk, first):
+            pair = slice(first, first + 2)
+            nc.vector.quantize_mx(
+                out=x_codes[blk][:, pair, :].rearrange("p g w -> p (g w)").bitcast(FP8X4),
+                scales=x_scales[blk][:, pair, :].rearrange("p g w -> p (g w)"),
+                in_=x_grouped[blk][:, pair, :].rearrange("p g c -> p (g c)"),
+            )
 
         tables = [keep.tile([P, TOKENS, 2], BF16, name="table%d" % side, align_bytes=64) for side in range(2)]
 
@@ -204,15 +203,16 @@ def tile_llamaattention_pa_kernel(
 
         idle_bank = psum.tile([P, TOKENS], F32, name="bank")
         keep_warm(idle_bank, 6)
-        transpose_x(0, idle_bank)
-        quantise_x(0)
+        transpose_x(0, idle_bank, (0, 2))
+        quantise_x(0, 0)
+        quantise_x(0, 2)
         make_tables()
-        idle_bank = psum.tile([P, TOKENS], F32, name="bank")
-        keep_warm(idle_bank, 2)
-        transpose_x(1, idle_bank)
-        keep_warm(idle_bank, 2)
         arrange_plane(0)
-        quantise_x(1)
+        idle_bank = psum.tile([P, TOKENS], F32, name="bank")
+        keep_warm(idle_bank, 1)
+        transpose_x(1, idle_bank, (0, 2))
+        quantise_x(1, 0)
+        quantise_x(1, 2)
 
         rot_codes = []
         rot_scales = []
@@ -224,6 +224,7 @@ def tile_llamaattention_pa_kernel(
             tok = slice(blk * BLOCK, (blk + 1) * BLOCK)
             products = []
             for half in range(2):
+
                 bank = psum.tile([P, PAIRS, BLOCK], F32, name="bank")
                 for pair in range(PAIRS):
                     first = (PAIRS * grp + pair) * CHUNK
@@ -281,15 +282,18 @@ def tile_llamaattention_pa_kernel(
 
         def finish(acc, t):
             result = results.tile([P, TOKENS], F32, name="result")
-            nc.vector.scalar_tensor_tensor(
-                out=result[:],
-                in0=acc[:],
-                scalar=1.0 / math.sqrt(CHUNK),
-                in1=mask_sb[:, t, :],
-                op0=MULT,
-                op1=ADD,
-            )
-            nc.sync.dma_start(out=out[0, t * P : (t + 1) * P, :], in_=result[:])
+            pieces = 2 if t == TOKEN_TILES - 1 else 1
+            for piece in range(pieces):
+                cols = slice(piece * TOKENS // pieces, (piece + 1) * TOKENS // pieces)
+                nc.vector.scalar_tensor_tensor(
+                    out=result[:, cols],
+                    in0=acc[:, cols],
+                    scalar=1.0 / math.sqrt(CHUNK),
+                    in1=mask_sb[:, t, cols],
+                    op0=MULT,
+                    op1=ADD,
+                )
+                nc.sync.dma_start(out=out[0, t * P : (t + 1) * P, cols], in_=result[:, cols])
 
         waiting = None
         for w in range(2):

@@ -48,9 +48,13 @@ def tile_llamaattention_pa_kernel(
         ident = keep.tile([P, P], F32)
         make_identity(nc, ident[:])
 
-        factors = keep.tile([P, TOKEN_TILES, 8 * HALF], BF16)
-        nc.sync.dma_start(out=factors[:, :, 2 * HALF : 4 * HALF], in_=cos.rearrange("(t p) f -> p t f", p=P))
-        nc.sync.dma_start(out=factors[:, :, 4 * HALF : 6 * HALF], in_=sin.rearrange("(t p) f -> p t f", p=P))
+        ident_bf16 = keep.tile([P, P], BF16)
+        nc.scalar.copy(out=ident_bf16[:], in_=ident[:])
+        cos_raw = keep.tile([P, TOKEN_TILES, CHUNK], BF16)
+        sin_raw = keep.tile([P, TOKEN_TILES, CHUNK], BF16)
+
+        def load_table(raw, table):
+            nc.sync.dma_start(out=raw[:], in_=table.rearrange("(p t) f -> p t f", t=TOKEN_TILES))
 
         zeros = keep.tile([P, TOKENS], BF16)
         nc.vector.memset(zeros[:], 0.0)
@@ -69,7 +73,7 @@ def tile_llamaattention_pa_kernel(
 
         def load_x(t):
             x_t = keep.tile([P, HIDDEN], BF16, name="x%d" % t)
-            nc.sync.dma_start(out=x_t[:], in_=hidden_states[0, t * P : (t + 1) * P, :])
+            nc.sync.dma_start(out=x_t[:], in_=hidden_states[0].rearrange("(p t) k -> p t k", t=TOKEN_TILES)[:, t, :])
             x_sb.append(x_t)
 
         def load_scales(w):
@@ -111,7 +115,11 @@ def tile_llamaattention_pa_kernel(
             if last:
                 load_end(w, HIDDEN // 2 - HALF, HIDDEN - HALF)
 
-        for t in range(TOKEN_TILES):
+        for t in range(2):
+            load_x(t)
+        load_table(sin_raw, sin)
+        load_table(cos_raw, cos)
+        for t in range(2, TOKEN_TILES):
             load_x(t)
         load_scales(0)
         for grp in range(2):
@@ -123,17 +131,16 @@ def tile_llamaattention_pa_kernel(
             load_weights(1, grp)
 
         mask_sb = keep.tile([P, TOKEN_TILES, TOKENS], BF16)
-        nc.sync.dma_start(out=mask_sb[:], in_=attention_mask[0].rearrange("(t p) s -> p t s", p=P))
+        nc.sync.dma_start(out=mask_sb[:], in_=attention_mask[0].rearrange("(p t) s -> p t s", t=TOKEN_TILES))
 
+        slots = keep.tile([P, TOKEN_TILES, 6, HALF], BF16)
+        twice = [P, TOKEN_TILES, 2, HALF]
         nc.vector.tensor_scalar_mul(
-            out=factors[:, :, 0:HALF], in0=factors[:, :, 4 * HALF : 5 * HALF], scalar1=-1.0
+            out=slots[:, :, 0:3:2, :], in0=sin_raw[:, :, 0:HALF].unsqueeze(2).to_broadcast(twice), scalar1=-1.0
         )
-        table_src = keep.tile([P, TOKEN_TILES, 2, 2, HALF, 2], BF16)
-        for side in range(2):
-            first = 2 * HALF * (1 - side)
-            pairs = factors[:, :, first : first + 6 * HALF].rearrange("p t (h s) -> p t s h", h=2)[:, :, 0:HALF, :]
-            for table in range(2):
-                nc.vector.tensor_copy(out=table_src[:, :, table, 1 - side if table == 0 else side], in_=pairs)
+        nc.scalar.copy(out=slots[:, :, 4, :], in_=sin_raw[:, :, HALF:CHUNK])
+        nc.vector.tensor_copy(out=slots[:, :, 3:6:2, :], in_=cos_raw[:, :, HALF:CHUNK].unsqueeze(2).to_broadcast(twice))
+        nc.scalar.copy(out=slots[:, :, 1, :], in_=cos_raw[:, :, 0:HALF])
 
         x_grouped = []
         x_codes = []
@@ -174,18 +181,19 @@ def tile_llamaattention_pa_kernel(
                 in_=x_grouped[blk][:, pair, :].rearrange("p g c -> p (g c)"),
             )
 
-        tables = [keep.tile([P, TOKENS, 2], BF16, name="table%d" % side, align_bytes=64) for side in range(2)]
+        tables = [keep.tile([P, 2, TOKENS], BF16, name="table%d" % side, align_bytes=64) for side in range(2)]
 
-        def make_tables():
-            for side in range(2):
-                bank = psum.tile([P, TOKENS], F32, name="bank")
+        def make_table(side):
+            bank = psum.tile([P, 2, TOKENS], BF16, name="bank")
+            for h in range(2):
+                first = 3 * h + side
                 for t in range(TOKEN_TILES):
                     nc.tensor.transpose(
-                        out=bank[:, t * P : (t + 1) * P],
-                        in_=table_src[:, t, side].rearrange("p d i h -> p (d i h)").bitcast(F32),
-                        identity=ident[:],
+                        out=bank[:, h, t * P : (t + 1) * P],
+                        in_=slots[:, t, first : first + 2, :].rearrange("p s i -> p (s i)"),
+                        identity=ident_bf16[:],
                     )
-                nc.scalar.copy(out=tables[side][:].rearrange("p w h -> p (w h)").bitcast(F32), in_=bank[:])
+            nc.scalar.copy(out=tables[side][:], in_=bank[:])
 
         outer_scales = []
 
@@ -204,13 +212,14 @@ def tile_llamaattention_pa_kernel(
         idle_bank = psum.tile([P, TOKENS], F32, name="bank")
         keep_warm(idle_bank, 6)
         transpose_x(0, idle_bank, (0, 2))
+        make_table(0)
         quantise_x(0, 0)
         quantise_x(0, 2)
-        make_tables()
         arrange_plane(0)
         idle_bank = psum.tile([P, TOKENS], F32, name="bank")
         keep_warm(idle_bank, 1)
         transpose_x(1, idle_bank, (0, 2))
+        make_table(1)
         quantise_x(1, 0)
         quantise_x(1, 2)
 
@@ -247,7 +256,7 @@ def tile_llamaattention_pa_kernel(
                 nc.vector.tensor_tensor(
                     out=product[:],
                     in0=bank[:].rearrange("p r w -> p w r").unsqueeze(3).to_broadcast(shape),
-                    in1=tables[half][:, tok, :].unsqueeze(2).to_broadcast(shape),
+                    in1=tables[half][:, :, tok].rearrange("p h w -> p w h").unsqueeze(2).to_broadcast(shape),
                     op=MULT,
                 )
                 products.append(product)
@@ -281,19 +290,22 @@ def tile_llamaattention_pa_kernel(
             )
 
         def finish(acc, t):
-            result = results.tile([P, TOKENS], F32, name="result")
+            result = results.tile([P, TOKENS // TOKEN_TILES, TOKEN_TILES], F32, name="result")
+            sums = acc[:].rearrange("p (t m) -> p m t", t=TOKEN_TILES)
+            mask = mask_sb[:, t, :].rearrange("p (m t) -> p m t", t=TOKEN_TILES)
+            rows = out[0].rearrange("(p t) (m c) -> p t m c", t=TOKEN_TILES, c=TOKEN_TILES)
             pieces = 2 if t == TOKEN_TILES - 1 else 1
             for piece in range(pieces):
-                cols = slice(piece * TOKENS // pieces, (piece + 1) * TOKENS // pieces)
+                cols = slice(piece * P // pieces, (piece + 1) * P // pieces)
                 nc.vector.scalar_tensor_tensor(
-                    out=result[:, cols],
-                    in0=acc[:, cols],
+                    out=result[:, cols, :],
+                    in0=sums[:, cols, :],
                     scalar=1.0 / math.sqrt(CHUNK),
-                    in1=mask_sb[:, t, cols],
+                    in1=mask[:, cols, :],
                     op0=MULT,
                     op1=ADD,
                 )
-                nc.sync.dma_start(out=out[0, t * P : (t + 1) * P, cols], in_=result[:, cols])
+                nc.sync.dma_start(out=rows[:, t, cols, :], in_=result[:, cols, :])
 
         waiting = None
         for w in range(2):

@@ -135,12 +135,12 @@ def tile_llamaattention_pa_kernel(
 
         slots = keep.tile([P, TOKEN_TILES, 6, HALF], BF16)
         twice = [P, TOKEN_TILES, 2, HALF]
-        nc.vector.tensor_scalar_mul(
-            out=slots[:, :, 0:3:2, :], in0=sin_raw[:, :, 0:HALF].unsqueeze(2).to_broadcast(twice), scalar1=-1.0
+        nc.scalar.mul(
+            out=slots[:, :, 0:3:2, :], in_=sin_raw[:, :, 0:HALF].unsqueeze(2).to_broadcast(twice), mul=-1.0
         )
-        nc.scalar.copy(out=slots[:, :, 4, :], in_=sin_raw[:, :, HALF:CHUNK])
+        nc.vector.tensor_copy(out=slots[:, :, 4, :], in_=sin_raw[:, :, HALF:CHUNK])
+        nc.vector.tensor_copy(out=slots[:, :, 1, :], in_=cos_raw[:, :, 0:HALF])
         nc.vector.tensor_copy(out=slots[:, :, 3:6:2, :], in_=cos_raw[:, :, HALF:CHUNK].unsqueeze(2).to_broadcast(twice))
-        nc.scalar.copy(out=slots[:, :, 1, :], in_=cos_raw[:, :, 0:HALF])
 
         x_grouped = []
         x_codes = []
@@ -278,16 +278,35 @@ def tile_llamaattention_pa_kernel(
             )
 
         def score_pass(acc, t, grp):
-            rows = slice(t * P, (t + 1) * P)
+            blk, tile = divmod(t, TILES_PER_BLOCK)
+            pair, second = blk * BLOCKS + grp // 2, grp % 2
+            rows = slice(second * BLOCK + tile * P, second * BLOCK + (tile + 1) * P)
             nc.tensor.matmul_mx(
                 out=acc[:],
-                lhsT=rot_codes[1][:, grp, rows].bitcast(FP8X4),
-                lhsT_scale=rot_scales[1][:, grp, rows],
+                lhsT=rot_codes[1][:, pair, rows].bitcast(FP8X4),
+                lhsT_scale=rot_scales[1][:, pair, rows],
                 rhs=rot_codes[0][:, grp, :].bitcast(FP8X4),
                 rhs_scale=rot_scales[0][:, grp, :],
                 start=(grp == 0),
                 stop=(grp == GROUPS - 1),
             )
+
+        def scaled_scores(acc):
+            scaled = results.tile([P, TOKENS // TOKEN_TILES, TOKEN_TILES], F32, name="scaled")
+            nc.scalar.mul(
+                out=scaled[:], in_=acc[:].rearrange("p (t m) -> p m t", t=TOKEN_TILES), mul=1.0 / math.sqrt(CHUNK)
+            )
+            return scaled
+
+        def finish_off_vector(scaled, t):
+            bank = psum.tile([P, TOKENS], F32, name="bank")
+            nc.tensor.matmul(
+                bank[:], lhsT=ident[:], rhs=scaled[:].rearrange("p m c -> p (m c)"), start=True, stop=False
+            )
+            nc.tensor.matmul(bank[:], lhsT=ident_bf16[:], rhs=mask_sb[:, t, :], start=False, stop=True)
+            result = results.tile([P, TOKENS], F32, name="summed")
+            nc.scalar.copy(out=result[:], in_=bank[:])
+            nc.scalar.dma_start(out=out[0].rearrange("(p t) s -> p t s", t=TOKEN_TILES)[:, t, :], in_=result[:])
 
         def finish(acc, t):
             result = results.tile([P, TOKENS // TOKEN_TILES, TOKEN_TILES], F32, name="result")
@@ -309,31 +328,43 @@ def tile_llamaattention_pa_kernel(
 
         waiting = None
         for w in range(2):
-            for grp in range(GROUPS):
-                rotated = double.tile([P, BLOCKS, 4 * BLOCK], BF16, name="rotated", align_bytes=64)
-                add_products(nc.gpsimd, rotated, 0, project_and_multiply(w, grp, 0))
-                if (w, grp) == (0, 1):
+            for pair in range(GROUPS):
+                if w == 0:
+                    units = ((pair, 0), (pair, 1))
+                else:
+                    blk, half = divmod(pair, BLOCKS)
+                    units = ((2 * half, blk), (2 * half + 1, blk))
+                rotated = double.tile([P, 2, 4 * BLOCK], BF16, name="rotated", align_bytes=64)
+                add_products(nc.gpsimd, rotated, 0, project_and_multiply(w, *units[0]))
+                if (w, pair) == (0, 1):
                     arrange_plane(1)
-                last = (w, grp) == (1, GROUPS - 1)
+                last = (w, pair) == (1, GROUPS - 1)
                 if last:
                     quantise(*waiting)
-                products = project_and_multiply(w, grp, 1)
+                products = project_and_multiply(w, *units[1])
                 if not last:
                     if waiting is not None:
                         quantise(*waiting)
                     add_products(nc.gpsimd, rotated, 1, products)
-                    waiting = (w, grp, rotated)
+                    waiting = (w, pair, rotated)
 
         accs = [psum.tile([P, TOKENS], F32, name="bank") for t in range(TOKEN_TILES)]
-        for grp in range(GROUPS - 1):
-            for t in range(TOKEN_TILES):
+        for t in range(TILES_PER_BLOCK):
+            for grp in range(GROUPS):
+                score_pass(accs[t], t, grp)
+        scaled = [scaled_scores(accs[t]) for t in range(TILES_PER_BLOCK)]
+        for t in range(TILES_PER_BLOCK):
+            finish_off_vector(scaled[t], t)
+        for grp in range(GROUPS - 2):
+            for t in (2, 3):
                 score_pass(accs[t], t, grp)
         quantise(1, GROUPS - 1, rotated, 0, BLOCK)
         for t in (2, 3):
             add_products(nc.vector, rotated, 1, products, (t - 2) * P, P)
         for t in (2, 3):
             quantise(1, GROUPS - 1, rotated, t * P, P)
-        for t in range(TOKEN_TILES):
-            score_pass(accs[t], t, GROUPS - 1)
-        for t in range(TOKEN_TILES):
+        for grp in (GROUPS - 2, GROUPS - 1):
+            for t in (2, 3):
+                score_pass(accs[t], t, grp)
+        for t in (2, 3):
             finish(accs[t], t)

@@ -306,7 +306,7 @@ def tile_llamaattention_pa_kernel(
             nc.tensor.matmul(bank[:], lhsT=ident_bf16[:], rhs=mask_sb[:, t, :], start=False, stop=True)
             result = results.tile([P, TOKENS], F32, name="summed")
             nc.scalar.copy(out=result[:], in_=bank[:])
-            nc.scalar.dma_start(out=out[0].rearrange("(p t) s -> p t s", t=TOKEN_TILES)[:, t, :], in_=result[:])
+            nc.sync.dma_start(out=out[0].rearrange("(p t) s -> p t s", t=TOKEN_TILES)[:, t, :], in_=result[:])
 
         def finish(acc, t):
             result = results.tile([P, TOKENS // TOKEN_TILES, TOKEN_TILES], F32, name="result")
@@ -338,13 +338,10 @@ def tile_llamaattention_pa_kernel(
                 add_products(nc.gpsimd, rotated, 0, project_and_multiply(w, *units[0]))
                 if (w, pair) == (0, 1):
                     arrange_plane(1)
-                last = (w, pair) == (1, GROUPS - 1)
-                if last:
-                    quantise(*waiting)
                 products = project_and_multiply(w, *units[1])
-                if not last:
-                    if waiting is not None:
-                        quantise(*waiting)
+                if waiting is not None:
+                    quantise(*waiting)
+                if (w, pair) != (1, GROUPS - 1):
                     add_products(nc.gpsimd, rotated, 1, products)
                     waiting = (w, pair, rotated)
 

import math
from contextlib import ExitStack

import concourse.mybir as mybir
from concourse.masks import make_identity

F32 = mybir.dt.float32
BF16 = mybir.dt.bfloat16
I32 = mybir.dt.int32
U32 = mybir.dt.uint32
U8 = mybir.dt.uint8
FP8X4 = mybir.dt.float8_e4m3fn_x4
MULT = mybir.AluOpType.mult
ADD = mybir.AluOpType.add

P = 128
TOKENS = 512
HIDDEN = 2048
CHUNK = 128
HALF = CHUNK // 2
N_CHUNKS = HIDDEN // CHUNK
K_PASS = 4 * P
PASSES = HIDDEN // K_PASS
TOKEN_TILES = TOKENS // P
BLOCK = 256
BLOCKS = TOKENS // BLOCK
TILES_PER_BLOCK = BLOCK // P
GROUPS = PASSES
PAIRS = 2

FLOPS = 2 * (2 * TOKENS * HIDDEN * HIDDEN) + 2 * TOKENS * TOKENS * HIDDEN


def tile_llamaattention_pa_kernel(
    tc, hidden_states, wq_words, wq_scales, wk_words, wk_scales, cos, sin, attention_mask, out
):
    nc = tc.nc
    weights_dram = ((wk_words, wk_scales), (wq_words, wq_scales))

    with ExitStack() as ctx:
        keep = ctx.enter_context(tc.tile_pool(name="keep", bufs=1))
        work = ctx.enter_context(tc.tile_pool(name="work", bufs=3))
        double = ctx.enter_context(tc.tile_pool(name="double", bufs=2))
        results = ctx.enter_context(tc.tile_pool(name="results", bufs=TOKEN_TILES))
        psum = ctx.enter_context(tc.psum_pool(name="psum", bufs=8))
        ctx.enter_context(tc.manual_schedule())

        ident = keep.tile([P, P], F32)
        make_identity(nc, ident[:])

        ident_bf16 = keep.tile([P, P], BF16)
        nc.scalar.copy(out=ident_bf16[:], in_=ident[:])
        cos_raw = keep.tile([P, TOKEN_TILES, CHUNK], BF16)
        sin_raw = keep.tile([P, TOKEN_TILES, CHUNK], BF16)

        def load_table(raw, table):
            nc.sync.dma_start(out=raw[:], in_=table.rearrange("(p t) f -> p t f", t=TOKEN_TILES))

        zeros = keep.tile([P, TOKENS], BF16)
        nc.vector.memset(zeros[:], 0.0)

        def keep_warm(bank, count):
            for i in range(count):
                nc.tensor.matmul(bank[:], lhsT=zeros[:, 0:P], rhs=zeros[:], start=True, stop=True)

        staged = []
        for w in range(2):
            stage = keep.tile([P, HIDDEN], U8, name="stage%d" % w, align_bytes=64)
            nc.vector.memset(stage[:].bitcast(I32), 0)
            staged.append(stage)

        x_sb = []

        def load_x(t):
            x_t = keep.tile([P, HIDDEN], BF16, name="x%d" % t)
            nc.sync.dma_start(out=x_t[:], in_=hidden_states[0].rearrange("(p t) k -> p t k", t=TOKEN_TILES)[:, t, :])
            x_sb.append(x_t)

        def load_scales(w):
            for quad in range(4):
                nc.sync.dma_start(
                    out=staged[w][32 * quad : 32 * quad + 16, :].bitcast(I32),
                    in_=weights_dram[w][1][:, 4 * quad : 4 * quad + 4, :].bitcast(I32),
                )

        inner = [keep.tile([P, PASSES, HIDDEN // 2], U32, name="inner%d" % w, align_bytes=64) for w in range(2)]
        outer = [keep.tile([P, PASSES, HIDDEN // 2], U32, name="outer%d" % w, align_bytes=64) for w in range(2)]

        def load_runs(w, kp, tile, to, source, runs):
            words = weights_dram[w][0][kp].rearrange("p n t -> p (n t)").bitcast(I32)
            stop = source + (runs - 1) * 2 * CHUNK + CHUNK
            if runs > 1:
                in_ = words[:, source - HALF : source - HALF + runs * 2 * CHUNK]
                in_ = in_.rearrange("p (r s) -> p r s", r=runs)[:, :, HALF : HALF + CHUNK]
            else:
                in_ = words[:, source:stop].rearrange("p (r s) -> p r s", r=1)
            nc.sync.dma_start(
                out=tile[:, kp, to : to + runs * CHUNK].bitcast(I32).rearrange("p (r s) -> p r s", r=runs), in_=in_
            )

        def load_end(w, to, source):
            words = weights_dram[w][0].rearrange("g p n t -> p g (n t)").bitcast(I32)
            nc.sync.dma_start(
                out=outer[w][:, :, to : to + HALF].bitcast(I32), in_=words[:, :, source : source + HALF]
            )

        def load_weights(w, grp):
            for kp in range(PASSES):
                load_runs(w, kp, inner[w], 2 * CHUNK * grp, 4 * CHUNK * grp + HALF, 2)
            if grp == 0:
                load_end(w, 0, 0)
            last = grp == GROUPS - 1
            for kp in range(PASSES):
                load_runs(w, kp, outer[w], 2 * CHUNK * grp + HALF, 4 * CHUNK * grp + 3 * HALF, 1 if last else 2)
            if last:
                load_end(w, HIDDEN // 2 - HALF, HIDDEN - HALF)

        for t in range(2):
            load_x(t)
        load_table(sin_raw, sin)
        load_table(cos_raw, cos)
        for t in range(2, TOKEN_TILES):
            load_x(t)
        load_scales(0)
        for grp in range(2):
            load_weights(0, grp)
        load_scales(1)
        for grp in range(2, GROUPS):
            load_weights(0, grp)
        for grp in range(GROUPS):
            load_weights(1, grp)

        mask_sb = keep.tile([P, TOKEN_TILES, TOKENS], BF16)
        nc.sync.dma_start(out=mask_sb[:], in_=attention_mask[0].rearrange("(p t) s -> p t s", t=TOKEN_TILES))

        slots = keep.tile([P, TOKEN_TILES, 6, HALF], BF16)
        twice = [P, TOKEN_TILES, 2, HALF]
        nc.scalar.mul(
            out=slots[:, :, 0:3:2, :], in_=sin_raw[:, :, 0:HALF].unsqueeze(2).to_broadcast(twice), mul=-1.0
        )
        nc.vector.tensor_copy(out=slots[:, :, 4, :], in_=sin_raw[:, :, HALF:CHUNK])
        nc.vector.tensor_copy(out=slots[:, :, 1, :], in_=cos_raw[:, :, 0:HALF])
        nc.vector.tensor_copy(out=slots[:, :, 3:6:2, :], in_=cos_raw[:, :, HALF:CHUNK].unsqueeze(2).to_broadcast(twice))

        x_grouped = []
        x_codes = []
        x_scales = []

        def transpose_x(blk, idle_bank, vector_copies):
            banks = [psum.tile([P, 2, BLOCK], F32, name="bank") for kp in range(PASSES)]
            for tt in range(TILES_PER_BLOCK):
                if tt > 0:
                    keep_warm(idle_bank, TILES_PER_BLOCK - blk)
                x_words = x_sb[blk * TILES_PER_BLOCK + tt][:].bitcast(F32)
                for kp in range(PASSES):
                    for u in range(2):
                        nc.tensor.transpose(
                            out=banks[kp][:, u, tt * P : (tt + 1) * P],
                            in_=x_words[:, 256 * kp + u : 256 * (kp + 1) : 2],
                            identity=ident[:],
                        )
            grouped = keep.tile([P, PASSES, 4 * BLOCK], BF16, name="xg%d" % blk, align_bytes=64)
            for kp in range(PASSES):
                dst = grouped[:, kp, :].bitcast(F32).rearrange("p (w u) -> p w u", u=2)
                src = banks[kp][:].rearrange("p u w -> p w u")
                if kp in vector_copies:
                    nc.vector.tensor_copy(out=dst, in_=src)
                else:
                    nc.scalar.copy(out=dst, in_=src)
            x_grouped.append(grouped)

        for blk in range(BLOCKS):
            x_codes.append(keep.tile([P, PASSES, BLOCK], U32, name="xc%d" % blk, align_bytes=64))
            x_scales.append(keep.tile([P, PASSES, BLOCK], U8, name="xs%d" % blk, align_bytes=64))

        def quantise_x(blk, first):
            pair = slice(first, first + 2)
            nc.vector.quantize_mx(
                out=x_codes[blk][:, pair, :].rearrange("p g w -> p (g w)").bitcast(FP8X4),
                scales=x_scales[blk][:, pair, :].rearrange("p g w -> p (g w)"),
                in_=x_grouped[blk][:, pair, :].rearrange("p g c -> p (g c)"),
            )

        tables = [keep.tile([P, 2, TOKENS], BF16, name="table%d" % side, align_bytes=64) for side in range(2)]

        def make_table(side):
            bank = psum.tile([P, 2, TOKENS], BF16, name="bank")
            for h in range(2):
                first = 3 * h + side
                for t in range(TOKEN_TILES):
                    nc.tensor.transpose(
                        out=bank[:, h, t * P : (t + 1) * P],
                        in_=slots[:, t, first : first + 2, :].rearrange("p s i -> p (s i)"),
                        identity=ident_bf16[:],
                    )
            nc.scalar.copy(out=tables[side][:], in_=bank[:])

        outer_scales = []

        def arrange_plane(w):
            plane = keep.tile([P, HIDDEN // 2], U8, name="plane%d" % w, align_bytes=64)
            to = plane[:].bitcast(I32).rearrange("p (c i) -> p c i", i=HALF // 4)
            source = staged[w][:].bitcast(I32).rearrange("p (c i) -> p c i", i=HALF // 4)
            runs = N_CHUNKS // 2 - 1
            nc.vector.tensor_copy(
                out=to[:, 1 : 1 + 2 * runs].rearrange("p (r c) i -> p r (c i)", c=2),
                in_=source[:, 2 : 2 + 4 * runs].rearrange("p (r c) i -> p r (c i)", c=4)[:, :, HALF // 4 : 3 * (HALF // 4)],
            )
            nc.vector.tensor_copy(out=to[:, :: N_CHUNKS - 1], in_=source[:, :: 2 * N_CHUNKS - 1])
            outer_scales.append(plane)

        idle_bank = psum.tile([P, TOKENS], F32, name="bank")
        keep_warm(idle_bank, 6)
        transpose_x(0, idle_bank, (0, 2))
        make_table(0)
        quantise_x(0, 0)
        quantise_x(0, 2)
        arrange_plane(0)
        idle_bank = psum.tile([P, TOKENS], F32, name="bank")
        keep_warm(idle_bank, 1)
        transpose_x(1, idle_bank, (0, 2))
        make_table(1)
        quantise_x(1, 0)
        quantise_x(1, 2)

        rot_codes = []
        rot_scales = []
        for w in range(2):
            rot_codes.append(keep.tile([P, GROUPS, TOKENS], U32, name="rc%d" % w, align_bytes=64))
            rot_scales.append(keep.tile([P, GROUPS, TOKENS], U8, name="rs%d" % w, align_bytes=64))

        def project_and_multiply(w, grp, blk):
            tok = slice(blk * BLOCK, (blk + 1) * BLOCK)
            products = []
            for half in range(2):

                bank = psum.tile([P, PAIRS, BLOCK], F32, name="bank")
                for pair in range(PAIRS):
                    first = (PAIRS * grp + pair) * CHUNK
                    if half == 0:
                        weights, scales, first_scale = inner[w], staged[w], 2 * first + HALF
                    else:
                        weights, scales, first_scale = outer[w], outer_scales[w], first
                    for kp in range(PASSES):
                        nc.tensor.matmul_mx(
                            out=bank[:, pair, :],
                            lhsT=weights[:, kp, first : first + P].bitcast(FP8X4),
                            lhsT_scale=scales[4 * kp : P, first_scale : first_scale + P],
                            rhs=x_codes[blk][:, kp, :].bitcast(FP8X4),
                            rhs_scale=x_scales[blk][:, kp, :],
                            start=(kp == 0),
                            stop=(kp == PASSES - 1),
                        )
                product = work.tile([P, BLOCK, PAIRS, 2], F32, name="product%d" % half)
                shape = [P, BLOCK, PAIRS, 2]
                nc.vector.tensor_tensor(
                    out=product[:],
                    in0=bank[:].rearrange("p r w -> p w r").unsqueeze(3).to_broadcast(shape),
                    in1=tables[half][:, :, tok].rearrange("p h w -> p w h").unsqueeze(2).to_broadcast(shape),
                    op=MULT,
                )
                products.append(product)
            return products

        def add_products(engine, rotated, blk, products, first=0, count=BLOCK):
            engine.tensor_tensor(
                out=rotated[:, blk, 4 * first : 4 * (first + count)],
                in0=products[0][:, first : first + count].rearrange("p w r h -> p (w r h)"),
                in1=products[1][:, first : first + count].rearrange("p w r h -> p (w r h)"),
                op=ADD,
            )

        def quantise(w, grp, rotated, first=0, count=TOKENS):
            nc.vector.quantize_mx(
                out=rot_codes[w][:, grp, first : first + count].bitcast(FP8X4),
                scales=rot_scales[w][:, grp, first : first + count],
                in_=rotated[:].rearrange("p b c -> p (b c)")[:, 4 * first : 4 * (first + count)],
            )

        def score_pass(acc, t, grp):
            blk, tile = divmod(t, TILES_PER_BLOCK)
            pair, second = blk * BLOCKS + grp // 2, grp % 2
            rows = slice(second * BLOCK + tile * P, second * BLOCK + (tile + 1) * P)
            nc.tensor.matmul_mx(
                out=acc[:],
                lhsT=rot_codes[1][:, pair, rows].bitcast(FP8X4),
                lhsT_scale=rot_scales[1][:, pair, rows],
                rhs=rot_codes[0][:, grp, :].bitcast(FP8X4),
                rhs_scale=rot_scales[0][:, grp, :],
                start=(grp == 0),
                stop=(grp == GROUPS - 1),
            )

        def scaled_scores(acc):
            scaled = results.tile([P, TOKENS // TOKEN_TILES, TOKEN_TILES], F32, name="scaled")
            nc.scalar.mul(
                out=scaled[:], in_=acc[:].rearrange("p (t m) -> p m t", t=TOKEN_TILES), mul=1.0 / math.sqrt(CHUNK)
            )
            return scaled

        def finish_off_vector(scaled, t):
            bank = psum.tile([P, TOKENS], F32, name="bank")
            nc.tensor.matmul(
                bank[:], lhsT=ident[:], rhs=scaled[:].rearrange("p m c -> p (m c)"), start=True, stop=False
            )
            nc.tensor.matmul(bank[:], lhsT=ident_bf16[:], rhs=mask_sb[:, t, :], start=False, stop=True)
            result = results.tile([P, TOKENS], F32, name="summed")
            nc.scalar.copy(out=result[:], in_=bank[:])
            nc.sync.dma_start(out=out[0].rearrange("(p t) s -> p t s", t=TOKEN_TILES)[:, t, :], in_=result[:])

        def finish(acc, t):
            result = results.tile([P, TOKENS // TOKEN_TILES, TOKEN_TILES], F32, name="result")
            sums = acc[:].rearrange("p (t m) -> p m t", t=TOKEN_TILES)
            mask = mask_sb[:, t, :].rearrange("p (m t) -> p m t", t=TOKEN_TILES)
            rows = out[0].rearrange("(p t) (m c) -> p t m c", t=TOKEN_TILES, c=TOKEN_TILES)
            pieces = 2 if t == TOKEN_TILES - 1 else 1
            for piece in range(pieces):
                cols = slice(piece * P // pieces, (piece + 1) * P // pieces)
                nc.vector.scalar_tensor_tensor(
                    out=result[:, cols, :],
                    in0=sums[:, cols, :],
                    scalar=1.0 / math.sqrt(CHUNK),
                    in1=mask[:, cols, :],
                    op0=MULT,
                    op1=ADD,
                )
                nc.sync.dma_start(out=rows[:, t, cols, :], in_=result[:, cols, :])

        waiting = None
        for w in range(2):
            for pair in range(GROUPS):
                if w == 0:
                    units = ((pair, 0), (pair, 1))
                else:
                    blk, half = divmod(pair, BLOCKS)
                    units = ((2 * half, blk), (2 * half + 1, blk))
                rotated = double.tile([P, 2, 4 * BLOCK], BF16, name="rotated", align_bytes=64)
                add_products(nc.gpsimd, rotated, 0, project_and_multiply(w, *units[0]))
                if (w, pair) == (0, 1):
                    arrange_plane(1)
                products = project_and_multiply(w, *units[1])
                if waiting is not None:
                    quantise(*waiting)
                if (w, pair) != (1, GROUPS - 1):
                    add_products(nc.gpsimd, rotated, 1, products)
                    waiting = (w, pair, rotated)

        accs = [psum.tile([P, TOKENS], F32, name="bank") for t in range(TOKEN_TILES)]
        for t in range(TILES_PER_BLOCK):
            for grp in range(GROUPS):
                score_pass(accs[t], t, grp)
        scaled = [scaled_scores(accs[t]) for t in range(TILES_PER_BLOCK)]
        for t in range(TILES_PER_BLOCK):
            finish_off_vector(scaled[t], t)
        for grp in range(GROUPS - 2):
            for t in (2, 3):
                score_pass(accs[t], t, grp)
        quantise(1, GROUPS - 1, rotated, 0, BLOCK)
        for t in (2, 3):
            add_products(nc.vector, rotated, 1, products, (t - 2) * P, P)
        for t in (2, 3):
            quantise(1, GROUPS - 1, rotated, t * P, P)
        for grp in (GROUPS - 2, GROUPS - 1):
            for t in (2, 3):
                score_pass(accs[t], t, grp)
        for t in (2, 3):
            finish(accs[t], t)
